import numpy as np
import ml_dtypes

BF16 = ml_dtypes.bfloat16


def bf(x):
    return np.asarray(x, np.float32).astype(BF16)


def f32(x):
    return np.asarray(x, np.float32)


def f64(x):
    return np.asarray(x).astype(np.float64)


def striped(idx):
    return np.tile(idx.reshape(-1, 16).T, (8, 1))


H, L, E, S, N, C = 2, 256, 128, 2048, 128, 512


def setup_inputs():
    return {"base": f32(0.2 * np.random.standard_normal((C, S))), "q": bf(np.sqrt(2.0) * np.random.standard_normal((E, C))), "k": bf(np.sqrt(2.0) * np.random.standard_normal((E, H * N))), "offs": striped(np.random.permutation(S)[:N])}


def reference(base, q, k, offs):
    idx = offs[:16].T.reshape(-1)
    qh = f64(q).reshape(E, H, L)
    kh = f64(k).reshape(E, H, N)
    z = np.einsum("ehi,eht->hit", qh, kh) / np.sqrt(E)
    p = np.exp(z)
    r = 1.0 / p.sum(axis=-1, keepdims=True)
    out = f64(base).copy()
    out[:, idx] = (p * r).reshape(C, N)
    return out

@@ -1,0 +1,81 @@
+import math
+
+import concourse.mybir as mybir
+
+BF16, F32, U16 = mybir.dt.bfloat16, mybir.dt.float32, mybir.dt.uint16
+
+P = 128
+HEADS, QUERIES, FEATURES, PLACES, KEYS = 2, 256, 128, 2048, 128
+ROWS = HEADS * QUERIES
+BLOCKS = ROWS // P
+BLOCKS_PER_HEAD = QUERIES // P
+SCALE = 1.0 / math.sqrt(FEATURES)
+
+FLOPS = 2 * ROWS * KEYS * FEATURES
+
+
+def tile_dac_structure_kernel(tc, base, q, k, offs, out):
+    nc = tc.nc
+    with (
+        tc.tile_pool(name="held", bufs=1) as held,
+        tc.psum_pool(name="psum", bufs=1) as psum,
+    ):
+        offsets = held.tile([P, KEYS // 16], U16, name="offsets")
+        nc.sync.dma_start(offsets[:], offs)
+
+        q_sb = held.tile([FEATURES, ROWS], BF16, name="q_sb")
+        k_sb = held.tile([FEATURES, HEADS * KEYS], BF16, name="k_sb")
+        nc.scalar.dma_start(q_sb[:], q)
+        nc.scalar.dma_start(k_sb[:], k)
+
+        windows = []
+        for b in range(BLOCKS):
+            window = held.tile([P, PLACES], F32, name=f"window{b}")
+            nc.sync.dma_start(window[:], base[b * P : (b + 1) * P, :])
+            windows.append(window)
+
+        scores = psum.tile([P, BLOCKS * KEYS], F32, name="scores")
+        for b in range(BLOCKS):
+            h = b // BLOCKS_PER_HEAD
+            nc.tensor.matmul(
+                scores[:, b * KEYS : (b + 1) * KEYS],
+                q_sb[:, b * P : (b + 1) * P],
+                k_sb[:, h * KEYS : (h + 1) * KEYS],
+                start=True,
+                stop=True,
+            )
+
+        top = held.tile([P, BLOCKS], F32, name="top")
+        nc.vector.reduce_max(
+            top[:], scores[:].rearrange("p (b j) -> p b j", b=BLOCKS), axis=mybir.AxisListType.X
+        )
+        shift = held.tile([P, BLOCKS], F32, name="shift")
+        nc.vector.tensor_scalar_mul(shift[:], top[:], -SCALE)
+
+        p = held.tile([P, BLOCKS * KEYS], F32, name="p")
+        sums = held.tile([P, BLOCKS], F32, name="sums")
+        for b in range(BLOCKS):
+            nc.scalar.activation(
+                p[:, b * KEYS : (b + 1) * KEYS],
+                scores[:, b * KEYS : (b + 1) * KEYS],
+                mybir.ActivationFunctionType.Exp,
+                bias=shift[:, b : b + 1],
+                scale=SCALE,
+                accum_out=sums[:, b : b + 1],
+            )
+        r = held.tile([P, BLOCKS], F32, name="r")
+        nc.vector.reciprocal(r[:], sums[:])
+        r_wide = held.tile([P, BLOCKS * KEYS], F32, name="r_wide")
+        nc.vector.tensor_copy(
+            r_wide[:].rearrange("p (b j) -> p b j", b=BLOCKS),
+            r[:].unsqueeze(2).to_broadcast([P, BLOCKS, KEYS]),
+        )
+
+        for b in range(BLOCKS):
+            nc.vector.tensor_tensor(
+                windows[b][:].indirect(offsets[:]),
+                p[:, b * KEYS : (b + 1) * KEYS],
+                r_wide[:, b * KEYS : (b + 1) * KEYS],
+                mybir.AluOpType.mult,
+            )
+            nc.sync.dma_start(out[b * P : (b + 1) * P, :], windows[b][:])

@@ -78,4 +78,4 @@ def tile_dac_structure_kernel(tc, base, q, k, offs, out):
                 r_wide[:, b * KEYS : (b + 1) * KEYS],
                 mybir.AluOpType.mult,
             )
-            nc.sync.dma_start(out[b * P : (b + 1) * P, :], windows[b][:])
+            nc.scalar.dma_start(out[b * P : (b + 1) * P, :], windows[b][:])

@@ -20,9 +20,6 @@ def tile_dac_structure_kernel(tc, base, q, k, offs, out):
         tc.tile_pool(name="held", bufs=1) as held,
         tc.psum_pool(name="psum", bufs=1) as psum,
     ):
-        offsets = held.tile([P, KEYS // 16], U16, name="offsets")
-        nc.sync.dma_start(offsets[:], offs)
-
         q_sb = held.tile([FEATURES, ROWS], BF16, name="q_sb")
         k_sb = held.tile([FEATURES, HEADS * KEYS], BF16, name="k_sb")
         nc.scalar.dma_start(q_sb[:], q)
@@ -33,6 +30,9 @@ def tile_dac_structure_kernel(tc, base, q, k, offs, out):
             window = held.tile([P, PLACES], F32, name=f"window{b}")
             nc.sync.dma_start(window[:], base[b * P : (b + 1) * P, :])
             windows.append(window)
+            if b == 0:
+                offsets = held.tile([P, KEYS // 16], U16, name="offsets")
+                nc.sync.dma_start(offsets[:], offs)
 
         scores = psum.tile([P, BLOCKS * KEYS], F32, name="scores")
         for b in range(BLOCKS):
@@ -78,4 +78,4 @@ def tile_dac_structure_kernel(tc, base, q, k, offs, out):
                 r_wide[:, b * KEYS : (b + 1) * KEYS],
                 mybir.AluOpType.mult,
             )
-            nc.scalar.dma_start(out[b * P : (b + 1) * P, :], windows[b][:])
+            nc.sync.dma_start(out[b * P : (b + 1) * P, :], windows[b][:])

@@ -20,16 +20,17 @@ def tile_dac_structure_kernel(tc, base, q, k, offs, out):
         tc.tile_pool(name="held", bufs=1) as held,
         tc.psum_pool(name="psum", bufs=1) as psum,
     ):
+        windows = [
+            held.tile([P, PLACES], F32, name=f"window{b}", align_bytes=256) for b in range(BLOCKS)
+        ]
+
         q_sb = held.tile([FEATURES, ROWS], BF16, name="q_sb")
         k_sb = held.tile([FEATURES, HEADS * KEYS], BF16, name="k_sb")
         nc.scalar.dma_start(q_sb[:], q)
         nc.scalar.dma_start(k_sb[:], k)
 
-        windows = []
         for b in range(BLOCKS):
-            window = held.tile([P, PLACES], F32, name=f"window{b}")
-            nc.sync.dma_start(window[:], base[b * P : (b + 1) * P, :])
-            windows.append(window)
+            nc.sync.dma_start(windows[b][:], base[b * P : (b + 1) * P, :])
             if b == 0:
                 offsets = held.tile([P, KEYS // 16], U16, name="offsets")
                 nc.sync.dma_start(offsets[:], offs)

@@ -9,6 +9,7 @@ HEADS, QUERIES, FEATURES, PLACES, KEYS = 2, 256, 128, 2048, 128
 ROWS = HEADS * QUERIES
 BLOCKS = ROWS // P
 BLOCKS_PER_HEAD = QUERIES // P
+BANK = 512
 SCALE = 1.0 / math.sqrt(FEATURES)
 
 FLOPS = 2 * ROWS * KEYS * FEATURES
@@ -35,44 +36,44 @@ def tile_dac_structure_kernel(tc, base, q, k, offs, out):
                 offsets = held.tile([P, KEYS // 16], U16, name="offsets")
                 nc.sync.dma_start(offsets[:], offs)
 
-        scores = psum.tile([P, BLOCKS * KEYS], F32, name="scores")
+        scores = []
         for b in range(BLOCKS):
             h = b // BLOCKS_PER_HEAD
+            bank = psum.tile([P, BANK], F32, name=f"scores{b}")
             nc.tensor.matmul(
-                scores[:, b * KEYS : (b + 1) * KEYS],
+                bank[:, :KEYS],
                 q_sb[:, b * P : (b + 1) * P],
                 k_sb[:, h * KEYS : (h + 1) * KEYS],
                 start=True,
                 stop=True,
             )
+            scores.append(bank)
 
         top = held.tile([P, BLOCKS], F32, name="top")
-        nc.vector.reduce_max(
-            top[:], scores[:].rearrange("p (b j) -> p b j", b=BLOCKS), axis=mybir.AxisListType.X
-        )
         shift = held.tile([P, BLOCKS], F32, name="shift")
-        nc.vector.tensor_scalar_mul(shift[:], top[:], -SCALE)
-
         p = held.tile([P, BLOCKS * KEYS], F32, name="p")
         sums = held.tile([P, BLOCKS], F32, name="sums")
-        for b in range(BLOCKS):
+        r_wide = held.tile([P, BLOCKS * KEYS], F32, name="r_wide")
+
+        def exponentials(b):
+            nc.vector.reduce_max(
+                top[:, b : b + 1], scores[b][:, :KEYS], axis=mybir.AxisListType.X
+            )
+            nc.vector.tensor_scalar_mul(shift[:, b : b + 1], top[:, b : b + 1], -SCALE)
             nc.scalar.activation(
                 p[:, b * KEYS : (b + 1) * KEYS],
-                scores[:, b * KEYS : (b + 1) * KEYS],
+                scores[b][:, :KEYS],
                 mybir.ActivationFunctionType.Exp,
                 bias=shift[:, b : b + 1],
                 scale=SCALE,
                 accum_out=sums[:, b : b + 1],
             )
-        r = held.tile([P, BLOCKS], F32, name="r")
-        nc.vector.reciprocal(r[:], sums[:])
-        r_wide = held.tile([P, BLOCKS * KEYS], F32, name="r_wide")
-        nc.vector.tensor_copy(
-            r_wide[:].rearrange("p (b j) -> p b j", b=BLOCKS),
-            r[:].unsqueeze(2).to_broadcast([P, BLOCKS, KEYS]),
-        )
 
-        for b in range(BLOCKS):
+        def place(b):
+            nc.vector.reciprocal(
+                r_wide[:, b * KEYS : (b + 1) * KEYS],
+                sums[:, b : b + 1].to_broadcast([P, KEYS]),
+            )
             nc.vector.tensor_tensor(
                 windows[b][:].indirect(offsets[:]),
                 p[:, b * KEYS : (b + 1) * KEYS],
@@ -80,3 +81,9 @@ def tile_dac_structure_kernel(tc, base, q, k, offs, out):
                 mybir.AluOpType.mult,
             )
             nc.sync.dma_start(out[b * P : (b + 1) * P, :], windows[b][:])
+
+        exponentials(0)
+        for b in range(BLOCKS):
+            if b + 1 < BLOCKS:
+                exponentials(b + 1)
+            place(b)

import math

import concourse.mybir as mybir

BF16, F32, U16 = mybir.dt.bfloat16, mybir.dt.float32, mybir.dt.uint16

P = 128
HEADS, QUERIES, FEATURES, PLACES, KEYS = 2, 256, 128, 2048, 128
ROWS = HEADS * QUERIES
BLOCKS = ROWS // P
BLOCKS_PER_HEAD = QUERIES // P
BANK = 512
SCALE = 1.0 / math.sqrt(FEATURES)

FLOPS = 2 * ROWS * KEYS * FEATURES


def tile_dac_structure_kernel(tc, base, q, k, offs, out):
    nc = tc.nc
    with (
        tc.tile_pool(name="held", bufs=1) as held,
        tc.psum_pool(name="psum", bufs=1) as psum,
    ):
        windows = [
            held.tile([P, PLACES], F32, name=f"window{b}", align_bytes=256) for b in range(BLOCKS)
        ]

        q_sb = held.tile([FEATURES, ROWS], BF16, name="q_sb")
        k_sb = held.tile([FEATURES, HEADS * KEYS], BF16, name="k_sb")
        nc.scalar.dma_start(q_sb[:], q)
        nc.scalar.dma_start(k_sb[:], k)

        for b in range(BLOCKS):
            nc.sync.dma_start(windows[b][:], base[b * P : (b + 1) * P, :])
            if b == 0:
                offsets = held.tile([P, KEYS // 16], U16, name="offsets")
                nc.sync.dma_start(offsets[:], offs)

        scores = []
        for b in range(BLOCKS):
            h = b // BLOCKS_PER_HEAD
            bank = psum.tile([P, BANK], F32, name=f"scores{b}")
            nc.tensor.matmul(
                bank[:, :KEYS],
                q_sb[:, b * P : (b + 1) * P],
                k_sb[:, h * KEYS : (h + 1) * KEYS],
                start=True,
                stop=True,
            )
            scores.append(bank)

        top = held.tile([P, BLOCKS], F32, name="top")
        shift = held.tile([P, BLOCKS], F32, name="shift")
        p = held.tile([P, BLOCKS * KEYS], F32, name="p")
        sums = held.tile([P, BLOCKS], F32, name="sums")
        r_wide = held.tile([P, BLOCKS * KEYS], F32, name="r_wide")

        def exponentials(b):
            nc.vector.reduce_max(
                top[:, b : b + 1], scores[b][:, :KEYS], axis=mybir.AxisListType.X
            )
            nc.vector.tensor_scalar_mul(shift[:, b : b + 1], top[:, b : b + 1], -SCALE)
            nc.scalar.activation(
                p[:, b * KEYS : (b + 1) * KEYS],
                scores[b][:, :KEYS],
                mybir.ActivationFunctionType.Exp,
                bias=shift[:, b : b + 1],
                scale=SCALE,
                accum_out=sums[:, b : b + 1],
            )

        def place(b):
            nc.vector.reciprocal(
                r_wide[:, b * KEYS : (b + 1) * KEYS],
                sums[:, b : b + 1].to_broadcast([P, KEYS]),
            )
            nc.vector.tensor_tensor(
                windows[b][:].indirect(offsets[:]),
                p[:, b * KEYS : (b + 1) * KEYS],
                r_wide[:, b * KEYS : (b + 1) * KEYS],
                mybir.AluOpType.mult,
            )
            nc.sync.dma_start(out[b * P : (b + 1) * P, :], windows[b][:])

        exponentials(0)
        for b in range(BLOCKS):
            if b + 1 < BLOCKS:
                exponentials(b + 1)
            place(b)
